import numpy as np
import ml_dtypes


def mxq(x, axis, fmt="e4m3"):
    dtype, down = {"e4m3": (ml_dtypes.float8_e4m3fn, 7), "e5m2": (ml_dtypes.float8_e5m2, 14)}[fmt]
    v = np.moveaxis(np.asarray(x, np.float32).astype(ml_dtypes.bfloat16).astype(np.float64), axis, -1)
    blocks = v.reshape(v.shape[:-1] + (-1, 32))
    amax = np.abs(blocks).max(-1, keepdims=True)
    byte = np.maximum(np.where(amax > 0, np.frexp(amax)[1] - 1 + 127, 0) - down, 1)
    scale = np.exp2(byte - 127.0)
    codes = (blocks / scale).astype(np.float32).astype(dtype).astype(np.float64)
    return np.moveaxis((codes * scale).reshape(v.shape), -1, axis)


WIDE = False


def mx_kscale(k):
    if not WIDE:
        return np.ones(k)
    levels = np.array([10, -10, 5, -5, 0])
    a = np.random.permutation(np.resize(levels, k // 512 * 4)).reshape(k // 512, 4)
    idx = np.arange(k)
    return np.exp2(a[idx // 512, idx % 128 // 32])


BF16 = ml_dtypes.bfloat16


def bf(x):
    return np.asarray(x, np.float32).astype(BF16)


def f64(x):
    return np.asarray(x).astype(np.float64)


E2M1 = np.array([0.0, 0.5, 1.0, 1.5, 2.0, 3.0, 4.0, 6.0, -0.0, -0.5, -1.0, -1.5, -2.0, -3.0, -4.0, -6.0])


def pack_weight(w, fmt):
    k, n = w.shape
    w = f64(bf(w)).reshape(k // 32, 32, n)
    amax = np.abs(w).max(1)
    if fmt == "e4m3":
        byte = np.frexp(amax)[1] - 1 + 127 - 7
    else:
        mant, ex = np.frexp(amax / 6.0)
        byte = np.where(mant > 0.5, ex, ex - 1) + 127
    byte = np.clip(np.where(amax > 0, byte, 1), 1, 254)
    scaled = (w * np.exp2(127.0 - byte)[:, None, :]).reshape(k, n).astype(np.float32)
    by_word = np.ascontiguousarray(scaled.reshape(k // 512, 128, 4, n).transpose(0, 1, 3, 2))
    if fmt == "e4m3":
        words = by_word.astype(ml_dtypes.float8_e4m3fn).view(np.uint8)
    else:
        c = by_word.astype(ml_dtypes.float4_e2m1fn).view(np.uint8) & 0xF
        words = c[..., 0::2] | (c[..., 1::2] << 4)
    return np.ascontiguousarray(words), np.ascontiguousarray(byte.astype(np.uint8).reshape(k // 512, 16, n))


def unpack_weight(words, scales, fmt):
    g, p, n, _ = words.shape
    if fmt == "e4m3":
        vals = np.ascontiguousarray(words).view(ml_dtypes.float8_e4m3fn).astype(np.float64)
    else:
        nib = np.empty((g, p, n, 4), np.uint8)
        nib[..., 0::2] = words & 0xF
        nib[..., 1::2] = words >> 4
        vals = E2M1[nib]
    vals = vals * np.repeat(np.exp2(scales.astype(np.float64) - 127.0), 8, axis=1)[..., None]
    return vals.transpose(0, 1, 3, 2).reshape(g * 512, n)

def pack4(w):
    words, scales = pack_weight(w, "e2m1")
    return words.reshape(words.shape[0], 128, -1), scales


def unpack4(words, scales):
    return unpack_weight(words.reshape(words.shape[0], 128, -1, 2), scales, "e2m1")


T, B, I, H = 64, 128, 512, 128


def sigmoid(v):
    return 1.0 / (1.0 + np.exp(-v))


def setup_inputs():
    s = mx_kscale(I)
    input_seq = bf(np.random.standard_normal((T, B, I)) * s)
    w = np.random.standard_normal((3 * H, I)) / np.sqrt(I) / s[None, :]
    words, scales = pack4(np.ascontiguousarray(w.T))
    b_ih = bf(np.random.standard_normal(3 * H) * 0.3)
    gh = bf(np.random.standard_normal((B, 3 * H)) * 0.5)
    return {"input_seq": input_seq,
            "W_ih_words": words,
            "W_ih_scales": scales,
            "b_ih": b_ih,
            "gh": gh}


def reference(input_seq, W_ih_words, W_ih_scales, b_ih, gh):
    gi = (mxq(f64(input_seq), 2, "e4m3") @ unpack4(W_ih_words, W_ih_scales)) + f64(b_ih)
    g = f64(gh)
    i_r, i_z, i_n = gi[..., :H], gi[..., H:2 * H], gi[..., 2 * H:]
    h_r, h_z, h_n = g[..., :H], g[..., H:2 * H], g[..., 2 * H:]
    r = sigmoid(i_r + h_r)
    z = sigmoid(i_z + h_z)
    n = np.tanh(i_n + r * h_n)
    h = (1.0 - z) * n
    return np.transpose(h, (1, 0, 2))

@@ -1,0 +1,218 @@
+from contextlib import ExitStack
+
+import concourse.mybir as mybir
+from concourse.masks import make_identity
+
+F32 = mybir.dt.float32
+BF16 = mybir.dt.bfloat16
+I32 = mybir.dt.int32
+U32 = mybir.dt.uint32
+U8 = mybir.dt.uint8
+FP8X4 = mybir.dt.float8_e4m3fn_x4
+FP4X4 = mybir.dt.float4_e2m1fn_x4
+ACT = mybir.ActivationFunctionType
+ALU = mybir.AluOpType
+
+T, B, K, H = 64, 128, 512, 128
+P = 128
+GATES = 3
+HALVES = 2
+J = B // HALVES
+J_CHUNK = 4
+CHUNKS = J // J_CHUNK
+COLS = J_CHUNK * P
+WORDS = K // 2
+
+FLOPS = 2 * T * B * K * GATES * H
+
+
+def tile_grucellmodel_pa_t_kernel(tc, input_seq, W_ih_words, W_ih_scales, b_ih, gh, out):
+    nc = tc.nc
+    with ExitStack() as ctx:
+        consts = ctx.enter_context(tc.tile_pool(name="consts", bufs=1))
+        x_pool = ctx.enter_context(tc.tile_pool(name="x", bufs=CHUNKS))
+        mx_pool = ctx.enter_context(tc.tile_pool(name="mx", bufs=3))
+        gate_pool = ctx.enter_context(tc.tile_pool(name="gate", bufs=4))
+        psum_x = ctx.enter_context(tc.psum_pool(name="psum_x", bufs=2))
+        psum_rz = ctx.enter_context(tc.psum_pool(name="psum_rz", bufs=1))
+        psum_n = ctx.enter_context(tc.psum_pool(name="psum_n", bufs=2))
+        psum_o = ctx.enter_context(tc.psum_pool(name="psum_o", bufs=2))
+        ctx.enter_context(tc.manual_schedule())
+
+        x_rows = input_seq.rearrange("t (s j) k -> (t s) j k", s=HALVES)
+        x_tiles = []
+
+        def load_x(c):
+            x_sb = x_pool.tile([P, J_CHUNK, K], BF16)
+            nc.sync.dma_start(out=x_sb[:], in_=x_rows[:, J_CHUNK * c : J_CHUNK * (c + 1), :])
+            x_tiles.append(x_sb)
+
+        w_words = consts.tile([P, 2 * GATES * H], U8, align_bytes=64)
+        w_scales = consts.tile([P, GATES * H], U8, align_bytes=64)
+        nc.vector.memset(w_scales[:].bitcast(I32), 0)
+
+        load_x(0)
+        load_x(1)
+        nc.sync.dma_start(out=w_words[:].bitcast(I32), in_=W_ih_words[0].bitcast(I32))
+        for quad in range(4):
+            nc.sync.dma_start(
+                out=w_scales[32 * quad : 32 * quad + 4, :].bitcast(I32),
+                in_=W_ih_scales[0, 4 * quad : 4 * quad + 4, :].bitcast(I32),
+            )
+        for c in range(2, CHUNKS):
+            load_x(c)
+
+        small_bf = consts.tile([P, GATES + 1, H], BF16)
+        nc.vector.memset(small_bf[:, GATES, :], 0.0)
+        nc.scalar.dma_start(out=small_bf[:, 0:GATES, :], in_=gh.rearrange("b (g h) -> b g h", g=GATES))
+        nc.scalar.dma_start(out=small_bf[0:GATES, GATES, :], in_=b_ih.rearrange("(g h) -> g h", g=GATES))
+
+        ident = consts.tile([P, P], F32)
+        make_identity(nc, ident[:])
+
+        small_f32 = consts.tile([P, GATES + 1, H], F32)
+        nc.vector.tensor_copy(out=small_f32[:], in_=small_bf[:])
+        small_t = psum_o.tile([P, GATES + 1, P], F32, tag="h_rows")
+        for g in range(GATES + 1):
+            nc.tensor.transpose(small_t[:, g, :], small_f32[:, g, :], ident[:])
+        bias = consts.tile([P, GATES], F32)
+        nc.vector.tensor_copy(out=bias[:], in_=small_t[:, GATES, 0:GATES])
+        add_r = consts.tile([P, B], F32)
+        nc.vector.tensor_scalar(
+            out=add_r[:], in0=small_t[:, 0, :], scalar1=bias[:, 0:1], scalar2=None, op0=ALU.add
+        )
+        sub_z = consts.tile([P, B], F32)
+        nc.vector.tensor_scalar(
+            out=sub_z[:], in0=small_t[:, 1, :], scalar1=bias[:, 1:2], scalar2=-1.0, op0=ALU.add, op1=ALU.mult
+        )
+        gh_n = consts.tile([P, B], F32)
+        nc.vector.tensor_copy(out=gh_n[:], in_=small_t[:, 2, :])
+
+        grouped, codes, x_scales = {}, {}, {}
+        acc, r_gate, z_keep, cand, blend = {}, {}, {}, {}, {}
+
+        def by_batch(bank):
+            return bank[:].rearrange("h (j t s) -> h j t s", j=J_CHUNK, s=HALVES)
+
+        def transpose_x(c):
+            grouped_c = mx_pool.tile([P, J_CHUNK, P, 4], BF16, align_bytes=64, name="grouped")
+            as_words = (
+                grouped_c[:]
+                .rearrange("q j p v -> q (j p v)")
+                .bitcast(F32)
+                .rearrange("q (j p u) -> q j p u", j=J_CHUNK, u=2)
+            )
+            for pair in range(J_CHUNK // 2):
+                xt = psum_x.tile([P, 2, 2, P], F32)
+                for jj in range(2):
+                    row_words = x_tiles[c][:, 2 * pair + jj, :].bitcast(F32)
+                    for u in range(2):
+                        nc.tensor.transpose(xt[:, jj, u, :], row_words[:, u:WORDS:2], ident[:])
+                nc.vector.tensor_copy(
+                    out=as_words[:, 2 * pair : 2 * pair + 2, :, :],
+                    in_=xt[:].rearrange("q j u p -> q j p u"),
+                )
+            grouped[c] = grouped_c
+
+        def quantise(c):
+            codes_c = mx_pool.tile([P, COLS], U32, align_bytes=64, name="codes")
+            x_scales_c = mx_pool.tile([P, COLS], U8, align_bytes=64, name="x_scales")
+            nc.vector.quantize_mx(
+                out=codes_c[:].bitcast(FP8X4),
+                scales=x_scales_c[:],
+                in_=grouped[c][:].rearrange("q j p v -> q (j p v)"),
+            )
+            codes[c], x_scales[c] = codes_c, x_scales_c
+
+        def multiply(c):
+            acc_r = psum_rz.tile([P, COLS], F32)
+            acc_z = psum_rz.tile([P, COLS], F32)
+            acc_n = psum_n.tile([P, COLS], F32)
+            acc[c] = (acc_r, acc_z, acc_n)
+            for g in range(GATES):
+                nc.tensor.matmul_mx(
+                    out=acc[c][g][:],
+                    lhsT=w_words[:, 2 * H * g : 2 * H * (g + 1)].bitcast(FP4X4),
+                    lhsT_scale=w_scales[:, H * g : H * (g + 1)],
+                    rhs=codes[c][:].bitcast(FP8X4),
+                    rhs_scale=x_scales[c][:],
+                    start=True,
+                    stop=True,
+                )
+
+        def sigmoids(c):
+            r_c = gate_pool.tile([P, HALVES, J_CHUNK, T], F32, name="r_gate")
+            z_c = gate_pool.tile([P, HALVES, J_CHUNK, T], F32, name="z_keep")
+            for g, dst, addend, sign in ((0, r_c, add_r, 1.0), (1, z_c, sub_z, -1.0)):
+                for j in range(J_CHUNK):
+                    for s in range(HALVES):
+                        b = J * s + J_CHUNK * c + j
+                        nc.scalar.activation(
+                            out=dst[:, s, j, :],
+                            in_=by_batch(acc[c][g])[:, j, :, s],
+                            func=ACT.Sigmoid,
+                            bias=addend[:, b : b + 1],
+                            scale=sign,
+                        )
+            r_gate[c], z_keep[c] = r_c, z_c
+
+        def candidate_sum(c):
+            cand_c = gate_pool.tile([P, HALVES, J_CHUNK, T], F32, name="cand")
+            for j in range(J_CHUNK):
+                for s in range(HALVES):
+                    b = J * s + J_CHUNK * c + j
+                    nc.vector.scalar_tensor_tensor(
+                        out=cand_c[:, s, j, :],
+                        in0=r_gate[c][:, s, j, :],
+                        scalar=gh_n[:, b : b + 1],
+                        in1=by_batch(acc[c][2])[:, j, :, s],
+                        op0=ALU.mult,
+                        op1=ALU.add,
+                    )
+            cand[c] = cand_c
+
+        def tanh_and_blend(c):
+            n_c = gate_pool.tile([P, HALVES, J_CHUNK, T], F32, name="n_gate")
+            nc.scalar.activation(out=n_c[:], in_=cand[c][:], func=ACT.Tanh, bias=bias[:, 2:3], scale=1.0)
+            blend_c = gate_pool.tile([P, HALVES, J_CHUNK, T], F32, name="blend")
+            nc.gpsimd.tensor_tensor(out=blend_c[:], in0=z_keep[c][:], in1=n_c[:], op=ALU.mult)
+            blend[c] = blend_c
+
+        def transpose_h(c):
+            h_rows = psum_o.tile([P, HALVES, J_CHUNK // 2, H], F32)
+            for s in range(HALVES):
+                for pair in range(J_CHUNK // 2):
+                    nc.tensor.transpose(
+                        h_rows[:, s, pair, :],
+                        blend[c][:, s, 2 * pair : 2 * pair + 2, :].rearrange("h j t -> h (j t)"),
+                        ident[:],
+                    )
+            return h_rows
+
+        def store_h(c, h_rows):
+            h_sb = gate_pool.tile([P, HALVES, J_CHUNK // 2, H], F32)
+            nc.scalar.copy(out=h_sb[:], in_=h_rows[:])
+            for s in range(HALVES):
+                b0 = J * s + J_CHUNK * c
+                nc.sync.dma_start(
+                    out=out[b0 : b0 + J_CHUNK].rearrange("(pair jj) t h -> (jj t) pair h", jj=2),
+                    in_=h_sb[:, s, :, :],
+                )
+
+        for k in range(CHUNKS + 4):
+            h_rows = None
+            if k < CHUNKS:
+                transpose_x(k)
+            if k >= 4:
+                h_rows = transpose_h(k - 4)
+            if 1 <= k <= CHUNKS:
+                multiply(k - 1)
+                sigmoids(k - 1)
+            if 2 <= k <= CHUNKS + 1:
+                candidate_sum(k - 2)
+            if k < CHUNKS:
+                quantise(k)
+            if 2 <= k <= CHUNKS + 1:
+                tanh_and_blend(k - 2)
+            if k >= 4:
+                store_h(k - 4, h_rows)

@@ -18,19 +18,23 @@ P = 128
 GATES = 3
 HALVES = 2
 J = B // HALVES
-J_CHUNK = 4
-CHUNKS = J // J_CHUNK
-COLS = J_CHUNK * P
+PAIR = 2
 WORDS = K // 2
+PACK = 4
 
 FLOPS = 2 * T * B * K * GATES * H
 
 
+def chunk_list():
+    return [(j0, 2 * PAIR) for j0 in range(0, J, 2 * PAIR)]
+
+
 def tile_grucellmodel_pa_t_kernel(tc, input_seq, W_ih_words, W_ih_scales, b_ih, gh, out):
     nc = tc.nc
+    chunks = chunk_list()
     with ExitStack() as ctx:
         consts = ctx.enter_context(tc.tile_pool(name="consts", bufs=1))
-        x_pool = ctx.enter_context(tc.tile_pool(name="x", bufs=CHUNKS))
+        x_pool = ctx.enter_context(tc.tile_pool(name="x", bufs=J // PAIR))
         mx_pool = ctx.enter_context(tc.tile_pool(name="mx", bufs=3))
         gate_pool = ctx.enter_context(tc.tile_pool(name="gate", bufs=4))
         psum_x = ctx.enter_context(tc.psum_pool(name="psum_x", bufs=2))
@@ -42,25 +46,24 @@ def tile_grucellmodel_pa_t_kernel(tc, input_seq, W_ih_words, W_ih_scales, b_ih, 
         x_rows = input_seq.rearrange("t (s j) k -> (t s) j k", s=HALVES)
         x_tiles = []
 
-        def load_x(c):
-            x_sb = x_pool.tile([P, J_CHUNK, K], BF16)
-            nc.sync.dma_start(out=x_sb[:], in_=x_rows[:, J_CHUNK * c : J_CHUNK * (c + 1), :])
-            x_tiles.append(x_sb)
+        def load_x(first_load, last_load):
+            for i in range(first_load, last_load):
+                x_sb = x_pool.tile([P, PAIR, K], BF16)
+                nc.sync.dma_start(out=x_sb[:], in_=x_rows[:, PAIR * i : PAIR * (i + 1), :])
+                x_tiles.append(x_sb)
 
         w_words = consts.tile([P, 2 * GATES * H], U8, align_bytes=64)
         w_scales = consts.tile([P, GATES * H], U8, align_bytes=64)
         nc.vector.memset(w_scales[:].bitcast(I32), 0)
 
-        load_x(0)
-        load_x(1)
+        load_x(0, 2)
         nc.sync.dma_start(out=w_words[:].bitcast(I32), in_=W_ih_words[0].bitcast(I32))
         for quad in range(4):
             nc.sync.dma_start(
                 out=w_scales[32 * quad : 32 * quad + 4, :].bitcast(I32),
                 in_=W_ih_scales[0, 4 * quad : 4 * quad + 4, :].bitcast(I32),
             )
-        for c in range(2, CHUNKS):
-            load_x(c)
+        load_x(2, J // PAIR)
 
         small_bf = consts.tile([P, GATES + 1, H], BF16)
         nc.vector.memset(small_bf[:, GATES, :], 0.0)
@@ -70,53 +73,58 @@ def tile_grucellmodel_pa_t_kernel(tc, input_seq, W_ih_words, W_ih_scales, b_ih, 
         ident = consts.tile([P, P], F32)
         make_identity(nc, ident[:])
 
-        small_f32 = consts.tile([P, GATES + 1, H], F32)
-        nc.vector.tensor_copy(out=small_f32[:], in_=small_bf[:])
-        small_t = psum_o.tile([P, GATES + 1, P], F32, tag="h_rows")
-        for g in range(GATES + 1):
-            nc.tensor.transpose(small_t[:, g, :], small_f32[:, g, :], ident[:])
         bias = consts.tile([P, GATES], F32)
-        nc.vector.tensor_copy(out=bias[:], in_=small_t[:, GATES, 0:GATES])
+        minus_bias = consts.tile([P, GATES], F32)
         add_r = consts.tile([P, B], F32)
-        nc.vector.tensor_scalar(
-            out=add_r[:], in0=small_t[:, 0, :], scalar1=bias[:, 0:1], scalar2=None, op0=ALU.add
-        )
         sub_z = consts.tile([P, B], F32)
-        nc.vector.tensor_scalar(
-            out=sub_z[:], in0=small_t[:, 1, :], scalar1=bias[:, 1:2], scalar2=-1.0, op0=ALU.add, op1=ALU.mult
-        )
         gh_n = consts.tile([P, B], F32)
-        nc.vector.tensor_copy(out=gh_n[:], in_=small_t[:, 2, :])
+
+        def prepare_constants():
+            small_f32 = consts.tile([P, GATES + 1, H], F32)
+            nc.scalar.copy(out=small_f32[:], in_=small_bf[:])
+            small_t = psum_o.tile([P, GATES + 1, P], F32, tag="h_rows")
+            for g in range(GATES + 1):
+                nc.tensor.transpose(small_t[:, g, :], small_f32[:, g, :], ident[:])
+            nc.scalar.copy(out=bias[:], in_=small_t[:, GATES, 0:GATES])
+            nc.scalar.mul(minus_bias[:], bias[:], -1.0)
+            nc.scalar.activation(
+                out=add_r[:], in_=small_t[:, 0, :], func=ACT.Identity, bias=bias[:, 0:1], scale=1.0
+            )
+            nc.scalar.activation(
+                out=sub_z[:], in_=small_t[:, 1, :], func=ACT.Identity, bias=minus_bias[:, 1:2], scale=-1.0
+            )
+            nc.scalar.copy(out=gh_n[:], in_=small_t[:, 2, :])
 
         grouped, codes, x_scales = {}, {}, {}
         acc, r_gate, z_keep, cand, blend = {}, {}, {}, {}, {}
 
-        def by_batch(bank):
-            return bank[:].rearrange("h (j t s) -> h j t s", j=J_CHUNK, s=HALVES)
+        def by_batch(bank, nj):
+            return bank[:].rearrange("h (j t s) -> h j t s", j=nj, s=HALVES)
 
         def transpose_x(c):
-            grouped_c = mx_pool.tile([P, J_CHUNK, P, 4], BF16, align_bytes=64, name="grouped")
+            j0, nj = chunks[c]
+            grouped_c = mx_pool.tile([P, nj, P, PACK], BF16, align_bytes=64, name="grouped")
             as_words = (
                 grouped_c[:]
                 .rearrange("q j p v -> q (j p v)")
                 .bitcast(F32)
-                .rearrange("q (j p u) -> q j p u", j=J_CHUNK, u=2)
+                .rearrange("q (j p u) -> q j p u", j=nj, u=2)
             )
-            for pair in range(J_CHUNK // 2):
-                xt = psum_x.tile([P, 2, 2, P], F32)
-                for jj in range(2):
-                    row_words = x_tiles[c][:, 2 * pair + jj, :].bitcast(F32)
+            for j in range(0, nj, PAIR):
+                xt = psum_x.tile([P, PAIR, 2, P], F32)
+                for jj in range(PAIR):
+                    row_words = x_tiles[(j0 + j) // PAIR][:, jj, :].bitcast(F32)
                     for u in range(2):
                         nc.tensor.transpose(xt[:, jj, u, :], row_words[:, u:WORDS:2], ident[:])
                 nc.vector.tensor_copy(
-                    out=as_words[:, 2 * pair : 2 * pair + 2, :, :],
-                    in_=xt[:].rearrange("q j u p -> q j p u"),
+                    out=as_words[:, j : j + PAIR, :, :], in_=xt[:].rearrange("q j u p -> q j p u")
                 )
             grouped[c] = grouped_c
 
         def quantise(c):
-            codes_c = mx_pool.tile([P, COLS], U32, align_bytes=64, name="codes")
-            x_scales_c = mx_pool.tile([P, COLS], U8, align_bytes=64, name="x_scales")
+            nj = chunks[c][1]
+            codes_c = mx_pool.tile([P, nj * P], U32, align_bytes=64, name="codes")
+            x_scales_c = mx_pool.tile([P, nj * P], U8, align_bytes=64, name="x_scales")
             nc.vector.quantize_mx(
                 out=codes_c[:].bitcast(FP8X4),
                 scales=x_scales_c[:],
@@ -125,9 +133,10 @@ def tile_grucellmodel_pa_t_kernel(tc, input_seq, W_ih_words, W_ih_scales, b_ih, 
             codes[c], x_scales[c] = codes_c, x_scales_c
 
         def multiply(c):
-            acc_r = psum_rz.tile([P, COLS], F32)
-            acc_z = psum_rz.tile([P, COLS], F32)
-            acc_n = psum_n.tile([P, COLS], F32)
+            nj = chunks[c][1]
+            acc_r = psum_rz.tile([P, nj * P], F32)
+            acc_z = psum_rz.tile([P, nj * P], F32)
+            acc_n = psum_n.tile([P, nj * P], F32)
             acc[c] = (acc_r, acc_z, acc_n)
             for g in range(GATES):
                 nc.tensor.matmul_mx(
@@ -141,15 +150,16 @@ def tile_grucellmodel_pa_t_kernel(tc, input_seq, W_ih_words, W_ih_scales, b_ih, 
                 )
 
         def sigmoids(c):
-            r_c = gate_pool.tile([P, HALVES, J_CHUNK, T], F32, name="r_gate")
-            z_c = gate_pool.tile([P, HALVES, J_CHUNK, T], F32, name="z_keep")
+            j0, nj = chunks[c]
+            r_c = gate_pool.tile([P, HALVES, nj, T], F32, name="r_gate")
+            z_c = gate_pool.tile([P, HALVES, nj, T], F32, name="z_keep")
             for g, dst, addend, sign in ((0, r_c, add_r, 1.0), (1, z_c, sub_z, -1.0)):
-                for j in range(J_CHUNK):
+                for j in range(nj):
                     for s in range(HALVES):
-                        b = J * s + J_CHUNK * c + j
+                        b = J * s + j0 + j
                         nc.scalar.activation(
                             out=dst[:, s, j, :],
-                            in_=by_batch(acc[c][g])[:, j, :, s],
+                            in_=by_batch(acc[c][g], nj)[:, j, :, s],
                             func=ACT.Sigmoid,
                             bias=addend[:, b : b + 1],
                             scale=sign,
@@ -157,62 +167,69 @@ def tile_grucellmodel_pa_t_kernel(tc, input_seq, W_ih_words, W_ih_scales, b_ih, 
             r_gate[c], z_keep[c] = r_c, z_c
 
         def candidate_sum(c):
-            cand_c = gate_pool.tile([P, HALVES, J_CHUNK, T], F32, name="cand")
-            for j in range(J_CHUNK):
+            j0, nj = chunks[c]
+            cand_c = gate_pool.tile([P, HALVES, nj, T], F32, name="cand")
+            for j in range(nj):
                 for s in range(HALVES):
-                    b = J * s + J_CHUNK * c + j
+                    b = J * s + j0 + j
                     nc.vector.scalar_tensor_tensor(
                         out=cand_c[:, s, j, :],
                         in0=r_gate[c][:, s, j, :],
                         scalar=gh_n[:, b : b + 1],
-                        in1=by_batch(acc[c][2])[:, j, :, s],
+                        in1=by_batch(acc[c][2], nj)[:, j, :, s],
                         op0=ALU.mult,
                         op1=ALU.add,
                     )
             cand[c] = cand_c
 
         def tanh_and_blend(c):
-            n_c = gate_pool.tile([P, HALVES, J_CHUNK, T], F32, name="n_gate")
+            nj = chunks[c][1]
+            n_c = gate_pool.tile([P, HALVES, nj, T], F32, name="n_gate")
             nc.scalar.activation(out=n_c[:], in_=cand[c][:], func=ACT.Tanh, bias=bias[:, 2:3], scale=1.0)
-            blend_c = gate_pool.tile([P, HALVES, J_CHUNK, T], F32, name="blend")
+            blend_c = gate_pool.tile([P, HALVES, nj, T], F32, name="blend")
             nc.gpsimd.tensor_tensor(out=blend_c[:], in0=z_keep[c][:], in1=n_c[:], op=ALU.mult)
             blend[c] = blend_c
 
         def transpose_h(c):
-            h_rows = psum_o.tile([P, HALVES, J_CHUNK // 2, H], F32)
+            nj = chunks[c][1]
+            h_rows = psum_o.tile([P, HALVES, nj // PAIR, H], F32)
             for s in range(HALVES):
-                for pair in range(J_CHUNK // 2):
+                for j in range(0, nj, PAIR):
                     nc.tensor.transpose(
-                        h_rows[:, s, pair, :],
-                        blend[c][:, s, 2 * pair : 2 * pair + 2, :].rearrange("h j t -> h (j t)"),
+                        h_rows[:, s, j // PAIR, :],
+                        blend[c][:, s, j : j + PAIR, :].rearrange("h j t -> h (j t)"),
                         ident[:],
                     )
             return h_rows
 
         def store_h(c, h_rows):
-            h_sb = gate_pool.tile([P, HALVES, J_CHUNK // 2, H], F32)
+            j0, nj = chunks[c]
+            h_sb = gate_pool.tile([P, HALVES, nj // PAIR, H], F32)
             nc.scalar.copy(out=h_sb[:], in_=h_rows[:])
             for s in range(HALVES):
-                b0 = J * s + J_CHUNK * c
+                b0 = J * s + j0
                 nc.sync.dma_start(
-                    out=out[b0 : b0 + J_CHUNK].rearrange("(pair jj) t h -> (jj t) pair h", jj=2),
+                    out=out[b0 : b0 + nj].rearrange("(pair jj) t h -> (jj t) pair h", jj=PAIR),
                     in_=h_sb[:, s, :, :],
                 )
 
-        for k in range(CHUNKS + 4):
+        n = len(chunks)
+        for k in range(n + 4):
             h_rows = None
-            if k < CHUNKS:
+            if k < n:
                 transpose_x(k)
+            if k == 0:
+                prepare_constants()
             if k >= 4:
                 h_rows = transpose_h(k - 4)
-            if 1 <= k <= CHUNKS:
+            if 1 <= k <= n:
                 multiply(k - 1)
                 sigmoids(k - 1)
-            if 2 <= k <= CHUNKS + 1:
+            if 2 <= k <= n + 1:
                 candidate_sum(k - 2)
-            if k < CHUNKS:
+            if k < n:
                 quantise(k)
-            if 2 <= k <= CHUNKS + 1:
+            if 2 <= k <= n + 1:
                 tanh_and_blend(k - 2)
             if k >= 4:
                 store_h(k - 4, h_rows)

@@ -73,6 +73,10 @@ def tile_grucellmodel_pa_t_kernel(tc, input_seq, W_ih_words, W_ih_scales, b_ih, 
         ident = consts.tile([P, P], F32)
         make_identity(nc, ident[:])
 
+        warm = consts.tile([P, 2], F32)
+        nc.vector.memset(warm[:, 0:1], 0.0)
+        nc.scalar.activation(out=warm[:, 1:2], in_=warm[:, 0:1], func=ACT.Sigmoid)
+
         bias = consts.tile([P, GATES], F32)
         minus_bias = consts.tile([P, GATES], F32)
         add_r = consts.tile([P, B], F32)

@@ -100,7 +100,7 @@ def tile_grucellmodel_pa_t_kernel(tc, input_seq, W_ih_words, W_ih_scales, b_ih, 
             nc.scalar.copy(out=gh_n[:], in_=small_t[:, 2, :])
 
         grouped, codes, x_scales = {}, {}, {}
-        acc, r_gate, z_keep, cand, blend = {}, {}, {}, {}, {}
+        acc, r_gate, z_keep, cand, n_gate, blend = {}, {}, {}, {}, {}, {}
 
         def by_batch(bank, nj):
             return bank[:].rearrange("h (j t s) -> h j t s", j=nj, s=HALVES)
@@ -186,12 +186,16 @@ def tile_grucellmodel_pa_t_kernel(tc, input_seq, W_ih_words, W_ih_scales, b_ih, 
                     )
             cand[c] = cand_c
 
-        def tanh_and_blend(c):
+        def tanh_gate(c):
             nj = chunks[c][1]
             n_c = gate_pool.tile([P, HALVES, nj, T], F32, name="n_gate")
             nc.scalar.activation(out=n_c[:], in_=cand[c][:], func=ACT.Tanh, bias=bias[:, 2:3], scale=1.0)
+            n_gate[c] = n_c
+
+        def blend_gates(c, engine):
+            nj = chunks[c][1]
             blend_c = gate_pool.tile([P, HALVES, nj, T], F32, name="blend")
-            nc.gpsimd.tensor_tensor(out=blend_c[:], in0=z_keep[c][:], in1=n_c[:], op=ALU.mult)
+            engine.tensor_tensor(out=blend_c[:], in0=z_keep[c][:], in1=n_gate[c][:], op=ALU.mult)
             blend[c] = blend_c
 
         def transpose_h(c):
@@ -206,10 +210,13 @@ def tile_grucellmodel_pa_t_kernel(tc, input_seq, W_ih_words, W_ih_scales, b_ih, 
                     )
             return h_rows
 
-        def store_h(c, h_rows):
+        def store_h(c, h_rows, on_vector):
             j0, nj = chunks[c]
             h_sb = gate_pool.tile([P, HALVES, nj // PAIR, H], F32)
-            nc.scalar.copy(out=h_sb[:], in_=h_rows[:])
+            if on_vector:
+                nc.vector.tensor_copy(out=h_sb[:], in_=h_rows[:])
+            else:
+                nc.scalar.copy(out=h_sb[:], in_=h_rows[:])
             for s in range(HALVES):
                 b0 = J * s + j0
                 nc.sync.dma_start(
@@ -218,22 +225,38 @@ def tile_grucellmodel_pa_t_kernel(tc, input_seq, W_ih_words, W_ih_scales, b_ih, 
                 )
 
         n = len(chunks)
-        for k in range(n + 4):
+        for k in range(n):
             h_rows = None
-            if k < n:
-                transpose_x(k)
+            transpose_x(k)
             if k == 0:
                 prepare_constants()
             if k >= 4:
                 h_rows = transpose_h(k - 4)
-            if 1 <= k <= n:
+            if k >= 1:
                 multiply(k - 1)
                 sigmoids(k - 1)
-            if 2 <= k <= n + 1:
+            if k >= 2:
                 candidate_sum(k - 2)
-            if k < n:
-                quantise(k)
-            if 2 <= k <= n + 1:
-                tanh_and_blend(k - 2)
+            quantise(k)
+            if k >= 2:
+                tanh_gate(k - 2)
+                blend_gates(k - 2, nc.gpsimd)
             if k >= 4:
-                store_h(k - 4, h_rows)
+                store_h(k - 4, h_rows, False)
+
+        h_rows = transpose_h(n - 4)
+        multiply(n - 1)
+        sigmoids(n - 1)
+        candidate_sum(n - 2)
+        store_h(n - 4, h_rows, True)
+        candidate_sum(n - 1)
+        tanh_gate(n - 2)
+        h_rows = transpose_h(n - 3)
+        store_h(n - 3, h_rows, True)
+        blend_gates(n - 2, nc.vector)
+        tanh_gate(n - 1)
+        blend_gates(n - 1, nc.vector)
+        h_rows = transpose_h(n - 2)
+        store_h(n - 2, h_rows, False)
+        h_rows = transpose_h(n - 1)
+        store_h(n - 1, h_rows, True)

@@ -252,6 +252,15 @@ def tile_grucellmodel_pa_t_kernel(tc, input_seq, W_ih_words, W_ih_scales, b_ih, 
         candidate_sum(n - 1)
         tanh_gate(n - 2)
         h_rows = transpose_h(n - 3)
+        idle_bank = psum_x.tile([P, PAIR, 2, P], F32, name="xt")
+        for i in range(2):
+            nc.tensor.matmul(
+                out=idle_bank[:].rearrange("q j u p -> q (j u p)"),
+                lhsT=small_bf[:, 0, :],
+                rhs=small_bf[:].rearrange("b g h -> b (g h)"),
+                start=True,
+                stop=True,
+            )
         store_h(n - 3, h_rows, True)
         blend_gates(n - 2, nc.vector)
         tanh_gate(n - 1)

@@ -22,6 +22,8 @@ PAIR = 2
 WORDS = K // 2
 PACK = 4
 
+WARM_UP = 14
+
 FLOPS = 2 * T * B * K * GATES * H
 
 
@@ -52,6 +54,12 @@ def tile_grucellmodel_pa_t_kernel(tc, input_seq, W_ih_words, W_ih_scales, b_ih, 
                 nc.sync.dma_start(out=x_sb[:], in_=x_rows[:, PAIR * i : PAIR * (i + 1), :])
                 x_tiles.append(x_sb)
 
+        zeros = consts.tile([P, P], BF16)
+        nc.vector.memset(zeros[:], 0.0)
+        idle_bank = psum_n.tile([P, 4 * P], F32, name="acc_n")
+        for i in range(WARM_UP):
+            nc.tensor.matmul(out=idle_bank[:, 0:P], lhsT=zeros[:], rhs=zeros[:], start=True, stop=True)
+
         w_words = consts.tile([P, 2 * GATES * H], U8, align_bytes=64)
         w_scales = consts.tile([P, GATES * H], U8, align_bytes=64)
         nc.vector.memset(w_scales[:].bitcast(I32), 0)
@@ -72,6 +80,8 @@ def tile_grucellmodel_pa_t_kernel(tc, input_seq, W_ih_words, W_ih_scales, b_ih, 
 
         ident = consts.tile([P, P], F32)
         make_identity(nc, ident[:])
+        ident_bf = consts.tile([P, P], BF16)
+        make_identity(nc, ident_bf[:])
 
         warm = consts.tile([P, 2], F32)
         nc.vector.memset(warm[:, 0:1], 0.0)
@@ -84,11 +94,9 @@ def tile_grucellmodel_pa_t_kernel(tc, input_seq, W_ih_words, W_ih_scales, b_ih, 
         gh_n = consts.tile([P, B], F32)
 
         def prepare_constants():
-            small_f32 = consts.tile([P, GATES + 1, H], F32)
-            nc.scalar.copy(out=small_f32[:], in_=small_bf[:])
-            small_t = psum_o.tile([P, GATES + 1, P], F32, tag="h_rows")
+            small_t = psum_o.tile([P, GATES + 1, P], BF16, tag="h_rows")
             for g in range(GATES + 1):
-                nc.tensor.transpose(small_t[:, g, :], small_f32[:, g, :], ident[:])
+                nc.tensor.transpose(small_t[:, g, :], small_bf[:, g, :], ident_bf[:])
             nc.scalar.copy(out=bias[:], in_=small_t[:, GATES, 0:GATES])
             nc.scalar.mul(minus_bias[:], bias[:], -1.0)
             nc.scalar.activation(
@@ -120,9 +128,12 @@ def tile_grucellmodel_pa_t_kernel(tc, input_seq, W_ih_words, W_ih_scales, b_ih, 
                     row_words = x_tiles[(j0 + j) // PAIR][:, jj, :].bitcast(F32)
                     for u in range(2):
                         nc.tensor.transpose(xt[:, jj, u, :], row_words[:, u:WORDS:2], ident[:])
-                nc.vector.tensor_copy(
-                    out=as_words[:, j : j + PAIR, :, :], in_=xt[:].rearrange("q j u p -> q j p u")
-                )
+                words_c = as_words[:, j : j + PAIR, :, :]
+                planes = xt[:].rearrange("q j u p -> q j p u")
+                if c < 2 and j > 0:
+                    nc.scalar.copy(out=words_c, in_=planes)
+                else:
+                    nc.vector.tensor_copy(out=words_c, in_=planes)
             grouped[c] = grouped_c
 
         def quantise(c):
@@ -153,28 +164,27 @@ def tile_grucellmodel_pa_t_kernel(tc, input_seq, W_ih_words, W_ih_scales, b_ih, 
                     stop=True,
                 )
 
-        def sigmoids(c):
+        def sigmoid_gate(c, g):
             j0, nj = chunks[c]
-            r_c = gate_pool.tile([P, HALVES, nj, T], F32, name="r_gate")
-            z_c = gate_pool.tile([P, HALVES, nj, T], F32, name="z_keep")
-            for g, dst, addend, sign in ((0, r_c, add_r, 1.0), (1, z_c, sub_z, -1.0)):
+            gate, addend, sign = ((r_gate, add_r, 1.0), (z_keep, sub_z, -1.0))[g]
+            dst = gate_pool.tile([P, HALVES, nj, T], F32, name=("r_gate", "z_keep")[g])
+            for s in range(HALVES):
                 for j in range(nj):
-                    for s in range(HALVES):
-                        b = J * s + j0 + j
-                        nc.scalar.activation(
-                            out=dst[:, s, j, :],
-                            in_=by_batch(acc[c][g], nj)[:, j, :, s],
-                            func=ACT.Sigmoid,
-                            bias=addend[:, b : b + 1],
-                            scale=sign,
-                        )
-            r_gate[c], z_keep[c] = r_c, z_c
+                    b = J * s + j0 + j
+                    nc.scalar.activation(
+                        out=dst[:, s, j, :],
+                        in_=by_batch(acc[c][g], nj)[:, j, :, s],
+                        func=ACT.Sigmoid,
+                        bias=addend[:, b : b + 1],
+                        scale=sign,
+                    )
+            gate[c] = dst
 
         def candidate_sum(c):
             j0, nj = chunks[c]
             cand_c = gate_pool.tile([P, HALVES, nj, T], F32, name="cand")
-            for j in range(nj):
-                for s in range(HALVES):
+            for s in range(HALVES):
+                for j in range(nj):
                     b = J * s + j0 + j
                     nc.vector.scalar_tensor_tensor(
                         out=cand_c[:, s, j, :],
@@ -234,7 +244,8 @@ def tile_grucellmodel_pa_t_kernel(tc, input_seq, W_ih_words, W_ih_scales, b_ih, 
                 h_rows = transpose_h(k - 4)
             if k >= 1:
                 multiply(k - 1)
-                sigmoids(k - 1)
+                sigmoid_gate(k - 1, 0)
+                sigmoid_gate(k - 1, 1)
             if k >= 2:
                 candidate_sum(k - 2)
             quantise(k)
@@ -244,28 +255,55 @@ def tile_grucellmodel_pa_t_kernel(tc, input_seq, W_ih_words, W_ih_scales, b_ih, 
             if k >= 4:
                 store_h(k - 4, h_rows, False)
 
+        last = n - 1
+        nj = chunks[last][1]
+        pieces = [(s, slice(j, j + PAIR)) for s in range(HALVES) for j in range(0, nj, PAIR)]
+        multiply(last)
+        sigmoid_gate(last, 0)
         h_rows = transpose_h(n - 4)
-        multiply(n - 1)
-        sigmoids(n - 1)
         candidate_sum(n - 2)
-        store_h(n - 4, h_rows, True)
-        candidate_sum(n - 1)
         tanh_gate(n - 2)
+        sigmoid_gate(last, 1)
+        candidate_sum(last)
+        store_h(n - 4, h_rows, True)
         h_rows = transpose_h(n - 3)
-        idle_bank = psum_x.tile([P, PAIR, 2, P], F32, name="xt")
+        idle_bank = psum_n.tile([P, 4 * P], F32, name="acc_n")
         for i in range(2):
             nc.tensor.matmul(
-                out=idle_bank[:].rearrange("q j u p -> q (j u p)"),
+                out=idle_bank[:],
                 lhsT=small_bf[:, 0, :],
                 rhs=small_bf[:].rearrange("b g h -> b (g h)"),
                 start=True,
                 stop=True,
             )
-        store_h(n - 3, h_rows, True)
+        n_last = gate_pool.tile([P, HALVES, nj, T], F32, name="n_gate")
+        for s, js in pieces:
+            nc.scalar.activation(
+                out=n_last[:, s, js, :], in_=cand[last][:, s, js, :], func=ACT.Tanh, bias=bias[:, 2:3], scale=1.0
+            )
         blend_gates(n - 2, nc.vector)
-        tanh_gate(n - 1)
-        blend_gates(n - 1, nc.vector)
-        h_rows = transpose_h(n - 2)
-        store_h(n - 2, h_rows, False)
-        h_rows = transpose_h(n - 1)
-        store_h(n - 1, h_rows, True)
+        h_rows_2 = transpose_h(n - 2)
+        store_h(n - 3, h_rows, False)
+        blend_last = gate_pool.tile([P, HALVES, nj, T], F32, name="blend")
+        banks = []
+        for s, js in pieces:
+            nc.vector.tensor_tensor(
+                out=blend_last[:, s, js, :], in0=z_keep[last][:, s, js, :], in1=n_last[:, s, js, :], op=ALU.mult
+            )
+            if js.start == 0:
+                banks.append(psum_x.tile([P, PAIR, 2, P], F32, name="xt"))
+            nc.tensor.transpose(
+                banks[s][:, js.start // PAIR, 0, :],
+                blend_last[:, s, js, :].rearrange("h j t -> h (j t)"),
+                ident[:],
+            )
+        h_last = gate_pool.tile([P, HALVES, nj // PAIR, H], F32, name="h_sb")
+        for s in range(HALVES):
+            nc.vector.tensor_copy(out=h_last[:, s, :, :], in_=banks[s][:, :, 0, :])
+            if s == 1:
+                store_h(n - 2, h_rows_2, False)
+            b0 = J * s + chunks[last][0]
+            nc.sync.dma_start(
+                out=out[b0 : b0 + nj].rearrange("(pair jj) t h -> (jj t) pair h", jj=PAIR),
+                in_=h_last[:, s, :, :],
+            )

@@ -257,15 +257,14 @@ def tile_grucellmodel_pa_t_kernel(tc, input_seq, W_ih_words, W_ih_scales, b_ih, 
 
         last = n - 1
         nj = chunks[last][1]
-        pieces = [(s, slice(j, j + PAIR)) for s in range(HALVES) for j in range(0, nj, PAIR)]
+        h_rows = transpose_h(n - 4)
         multiply(last)
         sigmoid_gate(last, 0)
-        h_rows = transpose_h(n - 4)
         candidate_sum(n - 2)
+        store_h(n - 4, h_rows, True)
         tanh_gate(n - 2)
         sigmoid_gate(last, 1)
         candidate_sum(last)
-        store_h(n - 4, h_rows, True)
         h_rows = transpose_h(n - 3)
         idle_bank = psum_n.tile([P, 4 * P], F32, name="acc_n")
         for i in range(2):
@@ -277,31 +276,30 @@ def tile_grucellmodel_pa_t_kernel(tc, input_seq, W_ih_words, W_ih_scales, b_ih, 
                 stop=True,
             )
         n_last = gate_pool.tile([P, HALVES, nj, T], F32, name="n_gate")
-        for s, js in pieces:
+        for s in range(HALVES):
             nc.scalar.activation(
-                out=n_last[:, s, js, :], in_=cand[last][:, s, js, :], func=ACT.Tanh, bias=bias[:, 2:3], scale=1.0
+                out=n_last[:, s, :, :], in_=cand[last][:, s, :, :], func=ACT.Tanh, bias=bias[:, 2:3], scale=1.0
             )
         blend_gates(n - 2, nc.vector)
+        store_h(n - 3, h_rows, True)
         h_rows_2 = transpose_h(n - 2)
-        store_h(n - 3, h_rows, False)
         blend_last = gate_pool.tile([P, HALVES, nj, T], F32, name="blend")
         banks = []
-        for s, js in pieces:
+        for s in range(HALVES):
             nc.vector.tensor_tensor(
-                out=blend_last[:, s, js, :], in0=z_keep[last][:, s, js, :], in1=n_last[:, s, js, :], op=ALU.mult
+                out=blend_last[:, s, :, :], in0=z_keep[last][:, s, :, :], in1=n_last[:, s, :, :], op=ALU.mult
             )
-            if js.start == 0:
-                banks.append(psum_x.tile([P, PAIR, 2, P], F32, name="xt"))
-            nc.tensor.transpose(
-                banks[s][:, js.start // PAIR, 0, :],
-                blend_last[:, s, js, :].rearrange("h j t -> h (j t)"),
-                ident[:],
-            )
+            banks.append(psum_x.tile([P, PAIR, 2, P], F32, name="xt"))
+            for j in range(0, nj, PAIR):
+                nc.tensor.transpose(
+                    banks[s][:, j // PAIR, 0, :],
+                    blend_last[:, s, j : j + PAIR, :].rearrange("h j t -> h (j t)"),
+                    ident[:],
+                )
         h_last = gate_pool.tile([P, HALVES, nj // PAIR, H], F32, name="h_sb")
+        store_h(n - 2, h_rows_2, False)
         for s in range(HALVES):
             nc.vector.tensor_copy(out=h_last[:, s, :, :], in_=banks[s][:, :, 0, :])
-            if s == 1:
-                store_h(n - 2, h_rows_2, False)
             b0 = J * s + chunks[last][0]
             nc.sync.dma_start(
                 out=out[b0 : b0 + nj].rearrange("(pair jj) t h -> (jj t) pair h", jj=PAIR),

from contextlib import ExitStack

import concourse.mybir as mybir
from concourse.masks import make_identity

F32 = mybir.dt.float32
BF16 = mybir.dt.bfloat16
I32 = mybir.dt.int32
U32 = mybir.dt.uint32
U8 = mybir.dt.uint8
FP8X4 = mybir.dt.float8_e4m3fn_x4
FP4X4 = mybir.dt.float4_e2m1fn_x4
ACT = mybir.ActivationFunctionType
ALU = mybir.AluOpType

T, B, K, H = 64, 128, 512, 128
P = 128
GATES = 3
HALVES = 2
J = B // HALVES
PAIR = 2
WORDS = K // 2
PACK = 4

WARM_UP = 14

FLOPS = 2 * T * B * K * GATES * H


def chunk_list():
    return [(j0, 2 * PAIR) for j0 in range(0, J, 2 * PAIR)]


def tile_grucellmodel_pa_t_kernel(tc, input_seq, W_ih_words, W_ih_scales, b_ih, gh, out):
    nc = tc.nc
    chunks = chunk_list()
    with ExitStack() as ctx:
        consts = ctx.enter_context(tc.tile_pool(name="consts", bufs=1))
        x_pool = ctx.enter_context(tc.tile_pool(name="x", bufs=J // PAIR))
        mx_pool = ctx.enter_context(tc.tile_pool(name="mx", bufs=3))
        gate_pool = ctx.enter_context(tc.tile_pool(name="gate", bufs=4))
        psum_x = ctx.enter_context(tc.psum_pool(name="psum_x", bufs=2))
        psum_rz = ctx.enter_context(tc.psum_pool(name="psum_rz", bufs=1))
        psum_n = ctx.enter_context(tc.psum_pool(name="psum_n", bufs=2))
        psum_o = ctx.enter_context(tc.psum_pool(name="psum_o", bufs=2))
        ctx.enter_context(tc.manual_schedule())

        x_rows = input_seq.rearrange("t (s j) k -> (t s) j k", s=HALVES)
        x_tiles = []

        def load_x(first_load, last_load):
            for i in range(first_load, last_load):
                x_sb = x_pool.tile([P, PAIR, K], BF16)
                nc.sync.dma_start(out=x_sb[:], in_=x_rows[:, PAIR * i : PAIR * (i + 1), :])
                x_tiles.append(x_sb)

        zeros = consts.tile([P, P], BF16)
        nc.vector.memset(zeros[:], 0.0)
        idle_bank = psum_n.tile([P, 4 * P], F32, name="acc_n")
        for i in range(WARM_UP):
            nc.tensor.matmul(out=idle_bank[:, 0:P], lhsT=zeros[:], rhs=zeros[:], start=True, stop=True)

        w_words = consts.tile([P, 2 * GATES * H], U8, align_bytes=64)
        w_scales = consts.tile([P, GATES * H], U8, align_bytes=64)
        nc.vector.memset(w_scales[:].bitcast(I32), 0)

        load_x(0, 2)
        nc.sync.dma_start(out=w_words[:].bitcast(I32), in_=W_ih_words[0].bitcast(I32))
        for quad in range(4):
            nc.sync.dma_start(
                out=w_scales[32 * quad : 32 * quad + 4, :].bitcast(I32),
                in_=W_ih_scales[0, 4 * quad : 4 * quad + 4, :].bitcast(I32),
            )
        load_x(2, J // PAIR)

        small_bf = consts.tile([P, GATES + 1, H], BF16)
        nc.vector.memset(small_bf[:, GATES, :], 0.0)
        nc.scalar.dma_start(out=small_bf[:, 0:GATES, :], in_=gh.rearrange("b (g h) -> b g h", g=GATES))
        nc.scalar.dma_start(out=small_bf[0:GATES, GATES, :], in_=b_ih.rearrange("(g h) -> g h", g=GATES))

        ident = consts.tile([P, P], F32)
        make_identity(nc, ident[:])
        ident_bf = consts.tile([P, P], BF16)
        make_identity(nc, ident_bf[:])

        warm = consts.tile([P, 2], F32)
        nc.vector.memset(warm[:, 0:1], 0.0)
        nc.scalar.activation(out=warm[:, 1:2], in_=warm[:, 0:1], func=ACT.Sigmoid)

        bias = consts.tile([P, GATES], F32)
        minus_bias = consts.tile([P, GATES], F32)
        add_r = consts.tile([P, B], F32)
        sub_z = consts.tile([P, B], F32)
        gh_n = consts.tile([P, B], F32)

        def prepare_constants():
            small_t = psum_o.tile([P, GATES + 1, P], BF16, tag="h_rows")
            for g in range(GATES + 1):
                nc.tensor.transpose(small_t[:, g, :], small_bf[:, g, :], ident_bf[:])
            nc.scalar.copy(out=bias[:], in_=small_t[:, GATES, 0:GATES])
            nc.scalar.mul(minus_bias[:], bias[:], -1.0)
            nc.scalar.activation(
                out=add_r[:], in_=small_t[:, 0, :], func=ACT.Identity, bias=bias[:, 0:1], scale=1.0
            )
            nc.scalar.activation(
                out=sub_z[:], in_=small_t[:, 1, :], func=ACT.Identity, bias=minus_bias[:, 1:2], scale=-1.0
            )
            nc.scalar.copy(out=gh_n[:], in_=small_t[:, 2, :])

        grouped, codes, x_scales = {}, {}, {}
        acc, r_gate, z_keep, cand, n_gate, blend = {}, {}, {}, {}, {}, {}

        def by_batch(bank, nj):
            return bank[:].rearrange("h (j t s) -> h j t s", j=nj, s=HALVES)

        def transpose_x(c):
            j0, nj = chunks[c]
            grouped_c = mx_pool.tile([P, nj, P, PACK], BF16, align_bytes=64, name="grouped")
            as_words = (
                grouped_c[:]
                .rearrange("q j p v -> q (j p v)")
                .bitcast(F32)
                .rearrange("q (j p u) -> q j p u", j=nj, u=2)
            )
            for j in range(0, nj, PAIR):
                xt = psum_x.tile([P, PAIR, 2, P], F32)
                for jj in range(PAIR):
                    row_words = x_tiles[(j0 + j) // PAIR][:, jj, :].bitcast(F32)
                    for u in range(2):
                        nc.tensor.transpose(xt[:, jj, u, :], row_words[:, u:WORDS:2], ident[:])
                words_c = as_words[:, j : j + PAIR, :, :]
                planes = xt[:].rearrange("q j u p -> q j p u")
                if c < 2 and j > 0:
                    nc.scalar.copy(out=words_c, in_=planes)
                else:
                    nc.vector.tensor_copy(out=words_c, in_=planes)
            grouped[c] = grouped_c

        def quantise(c):
            nj = chunks[c][1]
            codes_c = mx_pool.tile([P, nj * P], U32, align_bytes=64, name="codes")
            x_scales_c = mx_pool.tile([P, nj * P], U8, align_bytes=64, name="x_scales")
            nc.vector.quantize_mx(
                out=codes_c[:].bitcast(FP8X4),
                scales=x_scales_c[:],
                in_=grouped[c][:].rearrange("q j p v -> q (j p v)"),
            )
            codes[c], x_scales[c] = codes_c, x_scales_c

        def multiply(c):
            nj = chunks[c][1]
            acc_r = psum_rz.tile([P, nj * P], F32)
            acc_z = psum_rz.tile([P, nj * P], F32)
            acc_n = psum_n.tile([P, nj * P], F32)
            acc[c] = (acc_r, acc_z, acc_n)
            for g in range(GATES):
                nc.tensor.matmul_mx(
                    out=acc[c][g][:],
                    lhsT=w_words[:, 2 * H * g : 2 * H * (g + 1)].bitcast(FP4X4),
                    lhsT_scale=w_scales[:, H * g : H * (g + 1)],
                    rhs=codes[c][:].bitcast(FP8X4),
                    rhs_scale=x_scales[c][:],
                    start=True,
                    stop=True,
                )

        def sigmoid_gate(c, g):
            j0, nj = chunks[c]
            gate, addend, sign = ((r_gate, add_r, 1.0), (z_keep, sub_z, -1.0))[g]
            dst = gate_pool.tile([P, HALVES, nj, T], F32, name=("r_gate", "z_keep")[g])
            for s in range(HALVES):
                for j in range(nj):
                    b = J * s + j0 + j
                    nc.scalar.activation(
                        out=dst[:, s, j, :],
                        in_=by_batch(acc[c][g], nj)[:, j, :, s],
                        func=ACT.Sigmoid,
                        bias=addend[:, b : b + 1],
                        scale=sign,
                    )
            gate[c] = dst

        def candidate_sum(c):
            j0, nj = chunks[c]
            cand_c = gate_pool.tile([P, HALVES, nj, T], F32, name="cand")
            for s in range(HALVES):
                for j in range(nj):
                    b = J * s + j0 + j
                    nc.vector.scalar_tensor_tensor(
                        out=cand_c[:, s, j, :],
                        in0=r_gate[c][:, s, j, :],
                        scalar=gh_n[:, b : b + 1],
                        in1=by_batch(acc[c][2], nj)[:, j, :, s],
                        op0=ALU.mult,
                        op1=ALU.add,
                    )
            cand[c] = cand_c

        def tanh_gate(c):
            nj = chunks[c][1]
            n_c = gate_pool.tile([P, HALVES, nj, T], F32, name="n_gate")
            nc.scalar.activation(out=n_c[:], in_=cand[c][:], func=ACT.Tanh, bias=bias[:, 2:3], scale=1.0)
            n_gate[c] = n_c

        def blend_gates(c, engine):
            nj = chunks[c][1]
            blend_c = gate_pool.tile([P, HALVES, nj, T], F32, name="blend")
            engine.tensor_tensor(out=blend_c[:], in0=z_keep[c][:], in1=n_gate[c][:], op=ALU.mult)
            blend[c] = blend_c

        def transpose_h(c):
            nj = chunks[c][1]
            h_rows = psum_o.tile([P, HALVES, nj // PAIR, H], F32)
            for s in range(HALVES):
                for j in range(0, nj, PAIR):
                    nc.tensor.transpose(
                        h_rows[:, s, j // PAIR, :],
                        blend[c][:, s, j : j + PAIR, :].rearrange("h j t -> h (j t)"),
                        ident[:],
                    )
            return h_rows

        def store_h(c, h_rows, on_vector):
            j0, nj = chunks[c]
            h_sb = gate_pool.tile([P, HALVES, nj // PAIR, H], F32)
            if on_vector:
                nc.vector.tensor_copy(out=h_sb[:], in_=h_rows[:])
            else:
                nc.scalar.copy(out=h_sb[:], in_=h_rows[:])
            for s in range(HALVES):
                b0 = J * s + j0
                nc.sync.dma_start(
                    out=out[b0 : b0 + nj].rearrange("(pair jj) t h -> (jj t) pair h", jj=PAIR),
                    in_=h_sb[:, s, :, :],
                )

        n = len(chunks)
        for k in range(n):
            h_rows = None
            transpose_x(k)
            if k == 0:
                prepare_constants()
            if k >= 4:
                h_rows = transpose_h(k - 4)
            if k >= 1:
                multiply(k - 1)
                sigmoid_gate(k - 1, 0)
                sigmoid_gate(k - 1, 1)
            if k >= 2:
                candidate_sum(k - 2)
            quantise(k)
            if k >= 2:
                tanh_gate(k - 2)
                blend_gates(k - 2, nc.gpsimd)
            if k >= 4:
                store_h(k - 4, h_rows, False)

        last = n - 1
        nj = chunks[last][1]
        h_rows = transpose_h(n - 4)
        multiply(last)
        sigmoid_gate(last, 0)
        candidate_sum(n - 2)
        store_h(n - 4, h_rows, True)
        tanh_gate(n - 2)
        sigmoid_gate(last, 1)
        candidate_sum(last)
        h_rows = transpose_h(n - 3)
        idle_bank = psum_n.tile([P, 4 * P], F32, name="acc_n")
        for i in range(2):
            nc.tensor.matmul(
                out=idle_bank[:],
                lhsT=small_bf[:, 0, :],
                rhs=small_bf[:].rearrange("b g h -> b (g h)"),
                start=True,
                stop=True,
            )
        n_last = gate_pool.tile([P, HALVES, nj, T], F32, name="n_gate")
        for s in range(HALVES):
            nc.scalar.activation(
                out=n_last[:, s, :, :], in_=cand[last][:, s, :, :], func=ACT.Tanh, bias=bias[:, 2:3], scale=1.0
            )
        blend_gates(n - 2, nc.vector)
        store_h(n - 3, h_rows, True)
        h_rows_2 = transpose_h(n - 2)
        blend_last = gate_pool.tile([P, HALVES, nj, T], F32, name="blend")
        banks = []
        for s in range(HALVES):
            nc.vector.tensor_tensor(
                out=blend_last[:, s, :, :], in0=z_keep[last][:, s, :, :], in1=n_last[:, s, :, :], op=ALU.mult
            )
            banks.append(psum_x.tile([P, PAIR, 2, P], F32, name="xt"))
            for j in range(0, nj, PAIR):
                nc.tensor.transpose(
                    banks[s][:, j // PAIR, 0, :],
                    blend_last[:, s, j : j + PAIR, :].rearrange("h j t -> h (j t)"),
                    ident[:],
                )
        h_last = gate_pool.tile([P, HALVES, nj // PAIR, H], F32, name="h_sb")
        store_h(n - 2, h_rows_2, False)
        for s in range(HALVES):
            nc.vector.tensor_copy(out=h_last[:, s, :, :], in_=banks[s][:, :, 0, :])
            b0 = J * s + chunks[last][0]
            nc.sync.dma_start(
                out=out[b0 : b0 + nj].rearrange("(pair jj) t h -> (jj t) pair h", jj=PAIR),
                in_=h_last[:, s, :, :],
            )
